import numpy as np
import ml_dtypes


def mxq(x, axis, fmt="e4m3"):
    dtype, down = {"e4m3": (ml_dtypes.float8_e4m3fn, 7), "e5m2": (ml_dtypes.float8_e5m2, 14)}[fmt]
    v = np.moveaxis(np.asarray(x, np.float32).astype(ml_dtypes.bfloat16).astype(np.float64), axis, -1)
    blocks = v.reshape(v.shape[:-1] + (-1, 32))
    amax = np.abs(blocks).max(-1, keepdims=True)
    byte = np.maximum(np.where(amax > 0, np.frexp(amax)[1] - 1 + 127, 0) - down, 1)
    scale = np.exp2(byte - 127.0)
    codes = (blocks / scale).astype(np.float32).astype(dtype).astype(np.float64)
    return np.moveaxis((codes * scale).reshape(v.shape), -1, axis)


WIDE = False


def mx_kscale(k):
    if not WIDE:
        return np.ones(k)
    levels = np.array([10, -10, 5, -5, 0])
    a = np.random.permutation(np.resize(levels, k // 512 * 4)).reshape(k // 512, 4)
    idx = np.arange(k)
    return np.exp2(a[idx // 512, idx % 128 // 32])


BF16 = ml_dtypes.bfloat16


def bf(x):
    return np.asarray(x, np.float32).astype(BF16)


def f64(x):
    return np.asarray(x).astype(np.float64)


B, C, CK, H, W = 2, 1024, 512, 32, 32
N = H * W


def setup_inputs():
    s, t = mx_kscale(C), mx_kscale(CK)
    return {
        "x": bf(np.random.standard_normal((B, C, H, W)) * s[None, :, None, None]),
        "Wq": bf(np.random.standard_normal((CK, C)) / np.sqrt(C) / s[None, :] * t[:, None]),
        "bq": bf(np.random.standard_normal(CK) * 0.3 * t),
        "Wk": bf(np.random.standard_normal((CK, C)) / np.sqrt(C) / s[None, :] / t[:, None]),
        "bk": bf(np.random.standard_normal(CK) * 0.3 / t),
        "fg_sim": bf(np.random.uniform(size=(B, N, N))),
    }


def reference(x, Wq, bq, Wk, bk, fg_sim):
    xq = mxq(f64(x).reshape(B, C, N), 1, "e4m3")
    query = (mxq(f64(Wq), 1, "e4m3") @ xq).transpose(0, 2, 1) + f64(bq)
    key = (mxq(f64(Wk), 1, "e4m3") @ xq) + f64(bk)[None, :, None]
    sim = (mxq(query, 2, "e4m3") @ mxq(key, 1, "e4m3")) * CK ** -0.5
    return sim * f64(fg_sim)

@@ -1,0 +1,254 @@
+from contextlib import ExitStack
+
+import concourse.bass as bass
+import concourse.mybir as mybir
+import concourse.tile as tile
+from concourse.masks import make_identity
+
+F32 = mybir.dt.float32
+BF16 = mybir.dt.bfloat16
+U32 = mybir.dt.uint32
+U8 = mybir.dt.uint8
+FP8X4 = mybir.dt.float8_e4m3fn_x4
+ACT = mybir.ActivationFunctionType
+ALU = mybir.AluOpType
+
+P = 128
+B, C, CK, N = 2, 1024, 512, 1024
+HALF = 512
+FLOPS = 2 * B * (2 * CK * C * N + N * N * CK)
+
+X_ENG = {(0, 0, 0): "V", (0, 0, 1): "V", (0, 1, 0): "V", (0, 1, 1): "S",
+         (1, 0, 0): "V", (1, 1, 0): "V", (1, 0, 1): "S", (1, 1, 1): "S"}
+R_ENG = {(0, 1, 0): "V", (0, 1, 1): "V", (0, 0, 0): "V", (0, 0, 1): "V",
+         (1, 1, 0): "V", (1, 1, 1): "S", (1, 0, 0): "S", (1, 0, 1): "V"}
+Z_PER_ROUND = [0, 0, 0, 0, 2, 2, 2, 2]
+
+
+def tile_sgan_pa_kernel(tc, x, Wq, bq, Wk, bk, fg_sim, out):
+    nc = tc.nc
+    xf = x.rearrange("b c h w -> b c (h w)")
+    W = [Wq, Wk]
+    bias_dram = [bq, bk]
+
+    with ExitStack() as ctx:
+        keep = ctx.enter_context(tc.tile_pool(name="keep", bufs=1))
+        stage = ctx.enter_context(tc.tile_pool(name="stage", bufs=4))
+        outp = ctx.enter_context(tc.tile_pool(name="outp", bufs=4))
+        ps1 = ctx.enter_context(tc.psum_pool(name="ps1", bufs=4))
+        ps2 = ctx.enter_context(tc.psum_pool(name="ps2", bufs=4))
+
+        x_raw = {}
+        w_raw = {}
+        fg_sb = {}
+
+        def load_x(b, g):
+            t = keep.tile([P, 4 * N], BF16, name="xraw%d%d" % (b, g))
+            nc.sync.dma_start(
+                out=t[:].rearrange("p (u e n) -> p u e n", u=2, e=2),
+                in_=xf[b, HALF * g:HALF * (g + 1), :].rearrange("(u q e) n -> q u e n", u=2, e=2),
+            )
+            x_raw[(b, g)] = t
+
+        def load_w(w):
+            t = keep.tile([P, 4 * C], BF16, name="wraw%d" % w)
+            nc.sync.dma_start(
+                out=t[:].rearrange("p (t c) -> p t c", t=4),
+                in_=W[w].rearrange("(p t) c -> p t c", t=4),
+            )
+            w_raw[w] = t
+
+        def load_fg(b):
+            t = keep.tile([P, 8 * N], BF16, name="fg%d" % b)
+            nc.sync.dma_start(
+                out=t[:].rearrange("p (r i m) -> p r i m", r=2, i=4),
+                in_=fg_sim[b].rearrange("(r a i) m -> a r i m", r=2, i=4),
+            )
+            fg_sb[b] = t
+
+        bias_bf = []
+        for w in range(2):
+            t = keep.tile([P, 4], BF16, name="biasbf%d" % w)
+            nc.scalar.dma_start(out=t[:], in_=bias_dram[w].rearrange("(p t) -> p t", t=4))
+            bias_bf.append(t)
+
+        load_x(0, 0)
+        load_w(1)
+        load_x(0, 1)
+        load_w(0)
+        load_x(1, 0)
+        load_x(1, 1)
+        load_fg(0)
+        load_fg(1)
+
+        ident = keep.tile([P, P], F32, name="ident")
+        make_identity(nc, ident[:])
+        bias = []
+        for w in range(2):
+            t = keep.tile([P, 4], F32, name="bias%d" % w)
+            nc.vector.tensor_copy(out=t[:], in_=bias_bf[w][:])
+            bias.append(t)
+
+        def copy_on(eng, out_ap, in_ap):
+            if eng == "V":
+                nc.vector.tensor_copy(out=out_ap, in_=in_ap)
+            else:
+                nc.scalar.copy(out=out_ap, in_=in_ap)
+
+        def regroup(eng, dst, src):
+            copy_on(
+                eng,
+                dst[:].rearrange("p (c i s) -> p c s i", i=4, s=4),
+                src.rearrange("p s (c i) -> p c s i", i=4),
+            )
+
+        def quantise(name, grouped):
+            codes = keep.tile([P, HALF], U32, name="c_" + name, align_bytes=64)
+            scales = keep.tile([P, HALF], U8, name="s_" + name, align_bytes=64)
+            nc.vector.quantize_mx(out=codes[:].bitcast(FP8X4), scales=scales[:], in_=grouped[:])
+            return codes, scales
+
+        w_grp = {}
+        w_q = {}
+
+        def WU(w, g):
+            w32 = w_raw[w][:].bitcast(F32)
+            grp = stage.tile([P, 4 * HALF], BF16, name="wgrp", tag="wgrp", align_bytes=64)
+            g32 = grp[:].bitcast(F32).rearrange("p (c u) -> p c u", u=2)
+            for tp in range(2):
+                pw = ps1.tile([P, HALF], F32, name="pw", tag="bank1")
+                for tt in range(2):
+                    for u in range(2):
+                        col = 512 * (2 * tp + tt) + 256 * g + 128 * u
+                        nc.tensor.transpose(
+                            pw[:, (2 * tt + u) * P:(2 * tt + u + 1) * P],
+                            w32[:, col:col + P],
+                            ident[:],
+                        )
+                nc.scalar.copy(
+                    out=g32[:, 256 * tp:256 * (tp + 1), :].rearrange("p (tt j) u -> p tt j u", tt=2),
+                    in_=pw[:].rearrange("p (tt u j) -> p tt j u", tt=2, u=2),
+                )
+            w_grp[(w, g)] = grp
+
+        def WQ(w, g):
+            w_q[(w, g)] = quantise("w%d%d" % (w, g), w_grp[(w, g)])
+
+        x_grp = {}
+        x_q = {}
+
+        def XR(b, g, h):
+            grp = stage.tile([P, 4 * HALF], BF16, name="xgrp", tag="xgrp", align_bytes=64)
+            src = x_raw[(b, g)][:].rearrange("p (s n) -> p s n", s=4)[:, :, HALF * h:HALF * (h + 1)]
+            regroup(X_ENG[(b, g, h)], grp, src)
+            x_grp[(b, g, h)] = grp
+
+        def XQ(b, g, h):
+            x_q[(b, g, h)] = quantise("x%d%d%d" % (b, g, h), x_grp[(b, g, h)])
+
+        planes = {}
+        s_grp = {}
+        s_q = {}
+
+        def S1(b, w, h):
+            pl = stage.tile([P, 4 * HALF], BF16, name="planes", tag="planes")
+            plv = pl[:].rearrange("p (t n) -> p t n", t=4)
+            for t in range(4):
+                acc = ps1.tile([P, HALF], F32, name="acc1", tag="bank1")
+                for g in range(2):
+                    wc, ws = w_q[(w, g)]
+                    xc, xs = x_q[(b, g, h)]
+                    nc.tensor.matmul_mx(
+                        out=acc[:],
+                        lhsT=wc[:, P * t:P * (t + 1)].bitcast(FP8X4),
+                        lhsT_scale=ws[:, P * t:P * (t + 1)],
+                        rhs=xc[:].bitcast(FP8X4),
+                        rhs_scale=xs[:],
+                        start=(g == 0),
+                        stop=(g == 1),
+                    )
+                src = acc[:]
+                if w == 0:
+                    src = acc[:].rearrange("p (a i) -> p i a", i=4)
+                    dst = plv[:, t, :].rearrange("p (i a) -> p i a", i=4)
+                else:
+                    dst = plv[:, t, :]
+                nc.scalar.activation(out=dst, in_=src, func=ACT.Identity, bias=bias[w][:, t:t + 1], scale=1.0)
+            planes[(b, w, h)] = pl
+
+        def RR(b, w, h):
+            grp = stage.tile([P, 4 * HALF], BF16, name="sgrp", tag="sgrp", align_bytes=64)
+            regroup(R_ENG[(b, w, h)], grp, planes[(b, w, h)][:].rearrange("p (t n) -> p t n", t=4))
+            s_grp[(b, w, h)] = grp
+
+        def RQ(b, w, h):
+            s_q[(b, w, h)] = quantise("q%d%d%d" % (b, w, h), s_grp[(b, w, h)])
+
+        def S2(b, r, i):
+            o = outp.tile([P, N], F32, name="o")
+            qc, qs = s_q[(b, 0, r)]
+            fgv = fg_sb[b][:].rearrange("p (n m) -> p n m", n=8)
+            for hm in range(2):
+                kc, ks = s_q[(b, 1, hm)]
+                acc = ps2.tile([P, HALF], F32, name="acc2")
+                nc.tensor.matmul_mx(
+                    out=acc[:],
+                    lhsT=qc[:, P * i:P * (i + 1)].bitcast(FP8X4),
+                    lhsT_scale=qs[:, P * i:P * (i + 1)],
+                    rhs=kc[:].bitcast(FP8X4),
+                    rhs_scale=ks[:],
+                    start=True,
+                    stop=True,
+                )
+                nc.vector.scalar_tensor_tensor(
+                    out=o[:, HALF * hm:HALF * (hm + 1)],
+                    in0=acc[:],
+                    scalar=CK ** -0.5,
+                    in1=fgv[:, 4 * r + i, HALF * hm:HALF * (hm + 1)],
+                    op0=ALU.mult,
+                    op1=ALU.mult,
+                )
+            nc.sync.dma_start(
+                out=out[b].rearrange("(r a i) m -> a r i m", r=2, i=4)[:, r, i, :],
+                in_=o[:],
+            )
+
+        XR(0, 0, 0)
+        XR(0, 0, 1)
+        WU(1, 0)
+        WU(1, 1)
+        WQ(1, 0)
+        XQ(0, 0, 0)
+        WQ(1, 1)
+        XR(0, 1, 0)
+        XR(0, 1, 1)
+        XQ(0, 0, 1)
+        XQ(0, 1, 0)
+        XQ(0, 1, 1)
+        WU(0, 0)
+        WU(0, 1)
+        units = [(0, 1, 0), (0, 1, 1), (0, 0, 0), (0, 0, 1), (1, 1, 0), (1, 1, 1), (1, 0, 0), (1, 0, 1)]
+        x1 = [(1, 0, 0), (1, 1, 0), (1, 0, 1), (1, 1, 1)]
+        tiles = [(b, r, i) for b in range(2) for r in range(2) for i in range(4)]
+        done = 0
+        for k in range(8):
+            S1(*units[k])
+            if k == 0:
+                WQ(0, 0)
+                WQ(0, 1)
+            if k < 4:
+                XR(*x1[k])
+            if k >= 1:
+                RR(*units[k - 1])
+            if k < 4:
+                XQ(*x1[k])
+            if k >= 1:
+                RQ(*units[k - 1])
+            for z in range(Z_PER_ROUND[k]):
+                S2(*tiles[done])
+                done += 1
+        RR(*units[7])
+        RQ(*units[7])
+        while done < 16:
+            S2(*tiles[done])
+            done += 1

@@ -1,8 +1,6 @@
 from contextlib import ExitStack
 
-import concourse.bass as bass
 import concourse.mybir as mybir
-import concourse.tile as tile
 from concourse.masks import make_identity
 
 F32 = mybir.dt.float32
@@ -17,12 +15,9 @@ P = 128
 B, C, CK, N = 2, 1024, 512, 1024
 HALF = 512
 FLOPS = 2 * B * (2 * CK * C * N + N * N * CK)
-
-X_ENG = {(0, 0, 0): "V", (0, 0, 1): "V", (0, 1, 0): "V", (0, 1, 1): "S",
-         (1, 0, 0): "V", (1, 1, 0): "V", (1, 0, 1): "S", (1, 1, 1): "S"}
-R_ENG = {(0, 1, 0): "V", (0, 1, 1): "V", (0, 0, 0): "V", (0, 0, 1): "V",
-         (1, 1, 0): "V", (1, 1, 1): "S", (1, 0, 0): "S", (1, 0, 1): "V"}
-Z_PER_ROUND = [0, 0, 0, 0, 2, 2, 2, 2]
+PINNED = False
+Q = 0
+K = 1
 
 
 def tile_sgan_pa_kernel(tc, x, Wq, bq, Wk, bk, fg_sim, out):
@@ -32,9 +27,12 @@ def tile_sgan_pa_kernel(tc, x, Wq, bq, Wk, bk, fg_sim, out):
     bias_dram = [bq, bk]
 
     with ExitStack() as ctx:
+        if PINNED:
+            ctx.enter_context(tc.manual_schedule())
         keep = ctx.enter_context(tc.tile_pool(name="keep", bufs=1))
+        big = ctx.enter_context(tc.tile_pool(name="big", bufs=8))
         stage = ctx.enter_context(tc.tile_pool(name="stage", bufs=4))
-        outp = ctx.enter_context(tc.tile_pool(name="outp", bufs=4))
+        outp = ctx.enter_context(tc.tile_pool(name="outp", bufs=6))
         ps1 = ctx.enter_context(tc.psum_pool(name="ps1", bufs=4))
         ps2 = ctx.enter_context(tc.psum_pool(name="ps2", bufs=4))
 
@@ -43,7 +41,7 @@ def tile_sgan_pa_kernel(tc, x, Wq, bq, Wk, bk, fg_sim, out):
         fg_sb = {}
 
         def load_x(b, g):
-            t = keep.tile([P, 4 * N], BF16, name="xraw%d%d" % (b, g))
+            t = big.tile([P, 4 * N], BF16, name="xraw", tag="big")
             nc.sync.dma_start(
                 out=t[:].rearrange("p (u e n) -> p u e n", u=2, e=2),
                 in_=xf[b, HALF * g:HALF * (g + 1), :].rearrange("(u q e) n -> q u e n", u=2, e=2),
@@ -51,20 +49,20 @@ def tile_sgan_pa_kernel(tc, x, Wq, bq, Wk, bk, fg_sim, out):
             x_raw[(b, g)] = t
 
         def load_w(w):
-            t = keep.tile([P, 4 * C], BF16, name="wraw%d" % w)
+            t = big.tile([P, 4 * C], BF16, name="wraw", tag="big")
             nc.sync.dma_start(
                 out=t[:].rearrange("p (t c) -> p t c", t=4),
                 in_=W[w].rearrange("(p t) c -> p t c", t=4),
             )
             w_raw[w] = t
 
-        def load_fg(b):
-            t = keep.tile([P, 8 * N], BF16, name="fg%d" % b)
+        def load_fg(b, r):
+            t = big.tile([P, 4 * N], BF16, name="fg", tag="big")
             nc.sync.dma_start(
-                out=t[:].rearrange("p (r i m) -> p r i m", r=2, i=4),
-                in_=fg_sim[b].rearrange("(r a i) m -> a r i m", r=2, i=4),
+                out=t[:].rearrange("p (i m) -> p i m", i=4),
+                in_=fg_sim[b, HALF * r:HALF * (r + 1), :].rearrange("(a i) m -> a i m", i=4),
             )
-            fg_sb[b] = t
+            fg_sb[(b, r)] = t
 
         bias_bf = []
         for w in range(2):
@@ -72,14 +70,15 @@ def tile_sgan_pa_kernel(tc, x, Wq, bq, Wk, bk, fg_sim, out):
             nc.scalar.dma_start(out=t[:], in_=bias_dram[w].rearrange("(p t) -> p t", t=4))
             bias_bf.append(t)
 
+        load_w(K)
         load_x(0, 0)
-        load_w(1)
         load_x(0, 1)
-        load_w(0)
+        load_w(Q)
         load_x(1, 0)
         load_x(1, 1)
-        load_fg(0)
-        load_fg(1)
+        for b in range(B):
+            for r in range(2):
+                load_fg(b, r)
 
         ident = keep.tile([P, P], F32, name="ident")
         make_identity(nc, ident[:])
@@ -89,18 +88,13 @@ def tile_sgan_pa_kernel(tc, x, Wq, bq, Wk, bk, fg_sim, out):
             nc.vector.tensor_copy(out=t[:], in_=bias_bf[w][:])
             bias.append(t)
 
-        def copy_on(eng, out_ap, in_ap):
-            if eng == "V":
-                nc.vector.tensor_copy(out=out_ap, in_=in_ap)
+        def regroup(on_scalar, dst, src):
+            dst_v = dst[:].rearrange("p (c i s) -> p c s i", i=4, s=4)
+            src_v = src.rearrange("p s (c i) -> p c s i", i=4)
+            if on_scalar:
+                nc.scalar.copy(out=dst_v, in_=src_v)
             else:
-                nc.scalar.copy(out=out_ap, in_=in_ap)
-
-        def regroup(eng, dst, src):
-            copy_on(
-                eng,
-                dst[:].rearrange("p (c i s) -> p c s i", i=4, s=4),
-                src.rearrange("p s (c i) -> p c s i", i=4),
-            )
+                nc.vector.tensor_copy(out=dst_v, in_=src_v)
 
         def quantise(name, grouped):
             codes = keep.tile([P, HALF], U32, name="c_" + name, align_bytes=64)
@@ -113,7 +107,7 @@ def tile_sgan_pa_kernel(tc, x, Wq, bq, Wk, bk, fg_sim, out):
 
         def WU(w, g):
             w32 = w_raw[w][:].bitcast(F32)
-            grp = stage.tile([P, 4 * HALF], BF16, name="wgrp", tag="wgrp", align_bytes=64)
+            grp = stage.tile([P, 4 * HALF], BF16, name="wgrp", tag="wgrp", bufs=2, align_bytes=64)
             g32 = grp[:].bitcast(F32).rearrange("p (c u) -> p c u", u=2)
             for tp in range(2):
                 pw = ps1.tile([P, HALF], F32, name="pw", tag="bank1")
@@ -140,7 +134,7 @@ def tile_sgan_pa_kernel(tc, x, Wq, bq, Wk, bk, fg_sim, out):
         def XR(b, g, h):
             grp = stage.tile([P, 4 * HALF], BF16, name="xgrp", tag="xgrp", align_bytes=64)
             src = x_raw[(b, g)][:].rearrange("p (s n) -> p s n", s=4)[:, :, HALF * h:HALF * (h + 1)]
-            regroup(X_ENG[(b, g, h)], grp, src)
+            regroup(g == 1 and h == 1, grp, src)
             x_grp[(b, g, h)] = grp
 
         def XQ(b, g, h):
@@ -167,88 +161,100 @@ def tile_sgan_pa_kernel(tc, x, Wq, bq, Wk, bk, fg_sim, out):
                         start=(g == 0),
                         stop=(g == 1),
                     )
-                src = acc[:]
-                if w == 0:
+                if w == Q:
                     src = acc[:].rearrange("p (a i) -> p i a", i=4)
                     dst = plv[:, t, :].rearrange("p (i a) -> p i a", i=4)
                 else:
+                    src = acc[:]
                     dst = plv[:, t, :]
                 nc.scalar.activation(out=dst, in_=src, func=ACT.Identity, bias=bias[w][:, t:t + 1], scale=1.0)
             planes[(b, w, h)] = pl
 
         def RR(b, w, h):
             grp = stage.tile([P, 4 * HALF], BF16, name="sgrp", tag="sgrp", align_bytes=64)
-            regroup(R_ENG[(b, w, h)], grp, planes[(b, w, h)][:].rearrange("p (t n) -> p t n", t=4))
+            regroup(b == 1, grp, planes[(b, w, h)][:].rearrange("p (t n) -> p t n", t=4))
             s_grp[(b, w, h)] = grp
 
         def RQ(b, w, h):
             s_q[(b, w, h)] = quantise("q%d%d%d" % (b, w, h), s_grp[(b, w, h)])
 
-        def S2(b, r, i):
-            o = outp.tile([P, N], F32, name="o")
-            qc, qs = s_q[(b, 0, r)]
-            fgv = fg_sb[b][:].rearrange("p (n m) -> p n m", n=8)
-            for hm in range(2):
-                kc, ks = s_q[(b, 1, hm)]
-                acc = ps2.tile([P, HALF], F32, name="acc2")
-                nc.tensor.matmul_mx(
-                    out=acc[:],
-                    lhsT=qc[:, P * i:P * (i + 1)].bitcast(FP8X4),
-                    lhsT_scale=qs[:, P * i:P * (i + 1)],
-                    rhs=kc[:].bitcast(FP8X4),
-                    rhs_scale=ks[:],
-                    start=True,
-                    stop=True,
-                )
-                nc.vector.scalar_tensor_tensor(
-                    out=o[:, HALF * hm:HALF * (hm + 1)],
-                    in0=acc[:],
-                    scalar=CK ** -0.5,
-                    in1=fgv[:, 4 * r + i, HALF * hm:HALF * (hm + 1)],
-                    op0=ALU.mult,
-                    op1=ALU.mult,
-                )
-            nc.sync.dma_start(
-                out=out[b].rearrange("(r a i) m -> a r i m", r=2, i=4)[:, r, i, :],
-                in_=o[:],
-            )
+        o_tiles = {}
 
+        def S2(b, r, i, hm):
+            if (b, r, i) not in o_tiles:
+                o_tiles[(b, r, i)] = outp.tile([P, N], F32, name="o")
+            o = o_tiles[(b, r, i)]
+            qc, qs = s_q[(b, Q, r)]
+            kc, ks = s_q[(b, K, hm)]
+            acc = ps2.tile([P, HALF], F32, name="acc2")
+            nc.tensor.matmul_mx(
+                out=acc[:],
+                lhsT=qc[:, P * i:P * (i + 1)].bitcast(FP8X4),
+                lhsT_scale=qs[:, P * i:P * (i + 1)],
+                rhs=kc[:].bitcast(FP8X4),
+                rhs_scale=ks[:],
+                start=True,
+                stop=True,
+            )
+            nc.vector.scalar_tensor_tensor(
+                out=o[:, HALF * hm:HALF * (hm + 1)],
+                in0=acc[:],
+                scalar=CK ** -0.5,
+                in1=fg_sb[(b, r)][:, N * i + HALF * hm:N * i + HALF * (hm + 1)],
+                op0=ALU.mult,
+                op1=ALU.mult,
+            )
+            if hm == 1:
+                nc.sync.dma_start(
+                    out=out[b, HALF * r:HALF * (r + 1), :].rearrange("(a i) m -> a i m", i=4)[:, i, :],
+                    in_=o[:],
+                )
+
+        WU(K, 0)
+        WU(K, 1)
         XR(0, 0, 0)
+        WQ(K, 0)
         XR(0, 0, 1)
-        WU(1, 0)
-        WU(1, 1)
-        WQ(1, 0)
-        XQ(0, 0, 0)
-        WQ(1, 1)
+        WQ(K, 1)
         XR(0, 1, 0)
         XR(0, 1, 1)
-        XQ(0, 0, 1)
+        XQ(0, 0, 0)
         XQ(0, 1, 0)
+        XQ(0, 0, 1)
         XQ(0, 1, 1)
-        WU(0, 0)
-        WU(0, 1)
-        units = [(0, 1, 0), (0, 1, 1), (0, 0, 0), (0, 0, 1), (1, 1, 0), (1, 1, 1), (1, 0, 0), (1, 0, 1)]
-        x1 = [(1, 0, 0), (1, 1, 0), (1, 0, 1), (1, 1, 1)]
-        tiles = [(b, r, i) for b in range(2) for r in range(2) for i in range(4)]
-        done = 0
-        for k in range(8):
-            S1(*units[k])
+        WU(Q, 0)
+        WU(Q, 1)
+        units = [(b, w, h) for b in range(B) for h in range(2) for w in (K, Q)]
+        x1 = [(1, g, h) for h in range(2) for g in range(2)]
+        banks = []
+        for b in range(B):
+            banks += [(4 * b + 1, (b, 0, i, 0)) for i in range(4)]
+            banks += [(4 * b + 2, (b, 0, i, 1)) for i in range(4)]
+            banks += [(4 * b + 3, (b, 1, i, hm)) for i in range(4) for hm in range(2)]
+        issued = [0]
+
+        def stage2(count, quantised):
+            for z in range(count):
+                if issued[0] < len(banks) and banks[issued[0]][0] <= quantised:
+                    S2(*banks[issued[0]][1])
+                    issued[0] += 1
+
+        for k in range(9):
+            if k < 8:
+                S1(*units[k])
+                if units[k][0] == 1:
+                    RR(*units[k])
             if k == 0:
-                WQ(0, 0)
-                WQ(0, 1)
+                WQ(Q, 0)
+                WQ(Q, 1)
             if k < 4:
                 XR(*x1[k])
-            if k >= 1:
+            if 1 <= k <= 4:
                 RR(*units[k - 1])
-            if k < 4:
-                XQ(*x1[k])
+                XQ(*x1[k - 1])
+            if k == 8:
+                stage2(2, 6)
             if k >= 1:
                 RQ(*units[k - 1])
-            for z in range(Z_PER_ROUND[k]):
-                S2(*tiles[done])
-                done += 1
-        RR(*units[7])
-        RQ(*units[7])
-        while done < 16:
-            S2(*tiles[done])
-            done += 1
+            if k >= 3:
+                stage2(4 if k < 8 else 32, k - 1)

@@ -15,7 +15,7 @@ P = 128
 B, C, CK, N = 2, 1024, 512, 1024
 HALF = 512
 FLOPS = 2 * B * (2 * CK * C * N + N * N * CK)
-PINNED = False
+PINNED = True
 Q = 0
 K = 1
 

@@ -134,7 +134,7 @@ def tile_sgan_pa_kernel(tc, x, Wq, bq, Wk, bk, fg_sim, out):
         def XR(b, g, h):
             grp = stage.tile([P, 4 * HALF], BF16, name="xgrp", tag="xgrp", align_bytes=64)
             src = x_raw[(b, g)][:].rearrange("p (s n) -> p s n", s=4)[:, :, HALF * h:HALF * (h + 1)]
-            regroup(g == 1 and h == 1, grp, src)
+            regroup(b == 0 and g == 1 and h == 1, grp, src)
             x_grp[(b, g, h)] = grp
 
         def XQ(b, g, h):

@@ -32,7 +32,7 @@ def tile_sgan_pa_kernel(tc, x, Wq, bq, Wk, bk, fg_sim, out):
         keep = ctx.enter_context(tc.tile_pool(name="keep", bufs=1))
         big = ctx.enter_context(tc.tile_pool(name="big", bufs=8))
         stage = ctx.enter_context(tc.tile_pool(name="stage", bufs=4))
-        outp = ctx.enter_context(tc.tile_pool(name="outp", bufs=6))
+        outp = ctx.enter_context(tc.tile_pool(name="outp", bufs=8))
         ps1 = ctx.enter_context(tc.psum_pool(name="ps1", bufs=4))
         ps2 = ctx.enter_context(tc.psum_pool(name="ps2", bufs=4))
 
@@ -178,12 +178,8 @@ def tile_sgan_pa_kernel(tc, x, Wq, bq, Wk, bk, fg_sim, out):
         def RQ(b, w, h):
             s_q[(b, w, h)] = quantise("q%d%d%d" % (b, w, h), s_grp[(b, w, h)])
 
-        o_tiles = {}
-
         def S2(b, r, i, hm):
-            if (b, r, i) not in o_tiles:
-                o_tiles[(b, r, i)] = outp.tile([P, N], F32, name="o")
-            o = o_tiles[(b, r, i)]
+            o = outp.tile([P, HALF], F32, name="o")
             qc, qs = s_q[(b, Q, r)]
             kc, ks = s_q[(b, K, hm)]
             acc = ps2.tile([P, HALF], F32, name="acc2")
@@ -197,18 +193,17 @@ def tile_sgan_pa_kernel(tc, x, Wq, bq, Wk, bk, fg_sim, out):
                 stop=True,
             )
             nc.vector.scalar_tensor_tensor(
-                out=o[:, HALF * hm:HALF * (hm + 1)],
+                out=o[:],
                 in0=acc[:],
                 scalar=CK ** -0.5,
                 in1=fg_sb[(b, r)][:, N * i + HALF * hm:N * i + HALF * (hm + 1)],
                 op0=ALU.mult,
                 op1=ALU.mult,
             )
-            if hm == 1:
-                nc.sync.dma_start(
-                    out=out[b, HALF * r:HALF * (r + 1), :].rearrange("(a i) m -> a i m", i=4)[:, i, :],
-                    in_=o[:],
-                )
+            nc.sync.dma_start(
+                out=out[b, HALF * r:HALF * (r + 1), :].rearrange("(a i) m -> a i m", i=4)[:, i, HALF * hm:HALF * (hm + 1)],
+                in_=o[:],
+            )
 
         WU(K, 0)
         WU(K, 1)

from contextlib import ExitStack

import concourse.mybir as mybir
from concourse.masks import make_identity

F32 = mybir.dt.float32
BF16 = mybir.dt.bfloat16
U32 = mybir.dt.uint32
U8 = mybir.dt.uint8
FP8X4 = mybir.dt.float8_e4m3fn_x4
ACT = mybir.ActivationFunctionType
ALU = mybir.AluOpType

P = 128
B, C, CK, N = 2, 1024, 512, 1024
HALF = 512
FLOPS = 2 * B * (2 * CK * C * N + N * N * CK)
PINNED = True
Q = 0
K = 1


def tile_sgan_pa_kernel(tc, x, Wq, bq, Wk, bk, fg_sim, out):
    nc = tc.nc
    xf = x.rearrange("b c h w -> b c (h w)")
    W = [Wq, Wk]
    bias_dram = [bq, bk]

    with ExitStack() as ctx:
        if PINNED:
            ctx.enter_context(tc.manual_schedule())
        keep = ctx.enter_context(tc.tile_pool(name="keep", bufs=1))
        big = ctx.enter_context(tc.tile_pool(name="big", bufs=8))
        stage = ctx.enter_context(tc.tile_pool(name="stage", bufs=4))
        outp = ctx.enter_context(tc.tile_pool(name="outp", bufs=8))
        ps1 = ctx.enter_context(tc.psum_pool(name="ps1", bufs=4))
        ps2 = ctx.enter_context(tc.psum_pool(name="ps2", bufs=4))

        x_raw = {}
        w_raw = {}
        fg_sb = {}

        def load_x(b, g):
            t = big.tile([P, 4 * N], BF16, name="xraw", tag="big")
            nc.sync.dma_start(
                out=t[:].rearrange("p (u e n) -> p u e n", u=2, e=2),
                in_=xf[b, HALF * g:HALF * (g + 1), :].rearrange("(u q e) n -> q u e n", u=2, e=2),
            )
            x_raw[(b, g)] = t

        def load_w(w):
            t = big.tile([P, 4 * C], BF16, name="wraw", tag="big")
            nc.sync.dma_start(
                out=t[:].rearrange("p (t c) -> p t c", t=4),
                in_=W[w].rearrange("(p t) c -> p t c", t=4),
            )
            w_raw[w] = t

        def load_fg(b, r):
            t = big.tile([P, 4 * N], BF16, name="fg", tag="big")
            nc.sync.dma_start(
                out=t[:].rearrange("p (i m) -> p i m", i=4),
                in_=fg_sim[b, HALF * r:HALF * (r + 1), :].rearrange("(a i) m -> a i m", i=4),
            )
            fg_sb[(b, r)] = t

        bias_bf = []
        for w in range(2):
            t = keep.tile([P, 4], BF16, name="biasbf%d" % w)
            nc.scalar.dma_start(out=t[:], in_=bias_dram[w].rearrange("(p t) -> p t", t=4))
            bias_bf.append(t)

        load_w(K)
        load_x(0, 0)
        load_x(0, 1)
        load_w(Q)
        load_x(1, 0)
        load_x(1, 1)
        for b in range(B):
            for r in range(2):
                load_fg(b, r)

        ident = keep.tile([P, P], F32, name="ident")
        make_identity(nc, ident[:])
        bias = []
        for w in range(2):
            t = keep.tile([P, 4], F32, name="bias%d" % w)
            nc.vector.tensor_copy(out=t[:], in_=bias_bf[w][:])
            bias.append(t)

        def regroup(on_scalar, dst, src):
            dst_v = dst[:].rearrange("p (c i s) -> p c s i", i=4, s=4)
            src_v = src.rearrange("p s (c i) -> p c s i", i=4)
            if on_scalar:
                nc.scalar.copy(out=dst_v, in_=src_v)
            else:
                nc.vector.tensor_copy(out=dst_v, in_=src_v)

        def quantise(name, grouped):
            codes = keep.tile([P, HALF], U32, name="c_" + name, align_bytes=64)
            scales = keep.tile([P, HALF], U8, name="s_" + name, align_bytes=64)
            nc.vector.quantize_mx(out=codes[:].bitcast(FP8X4), scales=scales[:], in_=grouped[:])
            return codes, scales

        w_grp = {}
        w_q = {}

        def WU(w, g):
            w32 = w_raw[w][:].bitcast(F32)
            grp = stage.tile([P, 4 * HALF], BF16, name="wgrp", tag="wgrp", bufs=2, align_bytes=64)
            g32 = grp[:].bitcast(F32).rearrange("p (c u) -> p c u", u=2)
            for tp in range(2):
                pw = ps1.tile([P, HALF], F32, name="pw", tag="bank1")
                for tt in range(2):
                    for u in range(2):
                        col = 512 * (2 * tp + tt) + 256 * g + 128 * u
                        nc.tensor.transpose(
                            pw[:, (2 * tt + u) * P:(2 * tt + u + 1) * P],
                            w32[:, col:col + P],
                            ident[:],
                        )
                nc.scalar.copy(
                    out=g32[:, 256 * tp:256 * (tp + 1), :].rearrange("p (tt j) u -> p tt j u", tt=2),
                    in_=pw[:].rearrange("p (tt u j) -> p tt j u", tt=2, u=2),
                )
            w_grp[(w, g)] = grp

        def WQ(w, g):
            w_q[(w, g)] = quantise("w%d%d" % (w, g), w_grp[(w, g)])

        x_grp = {}
        x_q = {}

        def XR(b, g, h):
            grp = stage.tile([P, 4 * HALF], BF16, name="xgrp", tag="xgrp", align_bytes=64)
            src = x_raw[(b, g)][:].rearrange("p (s n) -> p s n", s=4)[:, :, HALF * h:HALF * (h + 1)]
            regroup(b == 0 and g == 1 and h == 1, grp, src)
            x_grp[(b, g, h)] = grp

        def XQ(b, g, h):
            x_q[(b, g, h)] = quantise("x%d%d%d" % (b, g, h), x_grp[(b, g, h)])

        planes = {}
        s_grp = {}
        s_q = {}

        def S1(b, w, h):
            pl = stage.tile([P, 4 * HALF], BF16, name="planes", tag="planes")
            plv = pl[:].rearrange("p (t n) -> p t n", t=4)
            for t in range(4):
                acc = ps1.tile([P, HALF], F32, name="acc1", tag="bank1")
                for g in range(2):
                    wc, ws = w_q[(w, g)]
                    xc, xs = x_q[(b, g, h)]
                    nc.tensor.matmul_mx(
                        out=acc[:],
                        lhsT=wc[:, P * t:P * (t + 1)].bitcast(FP8X4),
                        lhsT_scale=ws[:, P * t:P * (t + 1)],
                        rhs=xc[:].bitcast(FP8X4),
                        rhs_scale=xs[:],
                        start=(g == 0),
                        stop=(g == 1),
                    )
                if w == Q:
                    src = acc[:].rearrange("p (a i) -> p i a", i=4)
                    dst = plv[:, t, :].rearrange("p (i a) -> p i a", i=4)
                else:
                    src = acc[:]
                    dst = plv[:, t, :]
                nc.scalar.activation(out=dst, in_=src, func=ACT.Identity, bias=bias[w][:, t:t + 1], scale=1.0)
            planes[(b, w, h)] = pl

        def RR(b, w, h):
            grp = stage.tile([P, 4 * HALF], BF16, name="sgrp", tag="sgrp", align_bytes=64)
            regroup(b == 1, grp, planes[(b, w, h)][:].rearrange("p (t n) -> p t n", t=4))
            s_grp[(b, w, h)] = grp

        def RQ(b, w, h):
            s_q[(b, w, h)] = quantise("q%d%d%d" % (b, w, h), s_grp[(b, w, h)])

        def S2(b, r, i, hm):
            o = outp.tile([P, HALF], F32, name="o")
            qc, qs = s_q[(b, Q, r)]
            kc, ks = s_q[(b, K, hm)]
            acc = ps2.tile([P, HALF], F32, name="acc2")
            nc.tensor.matmul_mx(
                out=acc[:],
                lhsT=qc[:, P * i:P * (i + 1)].bitcast(FP8X4),
                lhsT_scale=qs[:, P * i:P * (i + 1)],
                rhs=kc[:].bitcast(FP8X4),
                rhs_scale=ks[:],
                start=True,
                stop=True,
            )
            nc.vector.scalar_tensor_tensor(
                out=o[:],
                in0=acc[:],
                scalar=CK ** -0.5,
                in1=fg_sb[(b, r)][:, N * i + HALF * hm:N * i + HALF * (hm + 1)],
                op0=ALU.mult,
                op1=ALU.mult,
            )
            nc.sync.dma_start(
                out=out[b, HALF * r:HALF * (r + 1), :].rearrange("(a i) m -> a i m", i=4)[:, i, HALF * hm:HALF * (hm + 1)],
                in_=o[:],
            )

        WU(K, 0)
        WU(K, 1)
        XR(0, 0, 0)
        WQ(K, 0)
        XR(0, 0, 1)
        WQ(K, 1)
        XR(0, 1, 0)
        XR(0, 1, 1)
        XQ(0, 0, 0)
        XQ(0, 1, 0)
        XQ(0, 0, 1)
        XQ(0, 1, 1)
        WU(Q, 0)
        WU(Q, 1)
        units = [(b, w, h) for b in range(B) for h in range(2) for w in (K, Q)]
        x1 = [(1, g, h) for h in range(2) for g in range(2)]
        banks = []
        for b in range(B):
            banks += [(4 * b + 1, (b, 0, i, 0)) for i in range(4)]
            banks += [(4 * b + 2, (b, 0, i, 1)) for i in range(4)]
            banks += [(4 * b + 3, (b, 1, i, hm)) for i in range(4) for hm in range(2)]
        issued = [0]

        def stage2(count, quantised):
            for z in range(count):
                if issued[0] < len(banks) and banks[issued[0]][0] <= quantised:
                    S2(*banks[issued[0]][1])
                    issued[0] += 1

        for k in range(9):
            if k < 8:
                S1(*units[k])
                if units[k][0] == 1:
                    RR(*units[k])
            if k == 0:
                WQ(Q, 0)
                WQ(Q, 1)
            if k < 4:
                XR(*x1[k])
            if 1 <= k <= 4:
                RR(*units[k - 1])
                XQ(*x1[k - 1])
            if k == 8:
                stage2(2, 6)
            if k >= 1:
                RQ(*units[k - 1])
            if k >= 3:
                stage2(4 if k < 8 else 32, k - 1)
